import numpy as np
import ml_dtypes


def mxq(x, axis, fmt="e4m3"):
    dtype, down = {"e4m3": (ml_dtypes.float8_e4m3fn, 7), "e5m2": (ml_dtypes.float8_e5m2, 14)}[fmt]
    v = np.moveaxis(np.asarray(x, np.float32).astype(ml_dtypes.bfloat16).astype(np.float64), axis, -1)
    blocks = v.reshape(v.shape[:-1] + (-1, 32))
    amax = np.abs(blocks).max(-1, keepdims=True)
    byte = np.maximum(np.where(amax > 0, np.frexp(amax)[1] - 1 + 127, 0) - down, 1)
    scale = np.exp2(byte - 127.0)
    codes = (blocks / scale).astype(np.float32).astype(dtype).astype(np.float64)
    return np.moveaxis((codes * scale).reshape(v.shape), -1, axis)


WIDE = False


def mx_kscale(k):
    if not WIDE:
        return np.ones(k)
    levels = np.array([10, -10, 5, -5, 0])
    a = np.random.permutation(np.resize(levels, k // 512 * 4)).reshape(k // 512, 4)
    idx = np.arange(k)
    return np.exp2(a[idx // 512, idx % 128 // 32])


BF16 = ml_dtypes.bfloat16


def bf(x):
    return np.asarray(x, np.float32).astype(BF16)


def f64(x):
    return np.asarray(x).astype(np.float64)


B, CQ, CR, HID, H, W = 2, 1024, 512, 512, 16, 32
P = H * W


def setup_inputs():
    s, r, t = mx_kscale(CQ), mx_kscale(CR), mx_kscale(HID)
    return {"query_features": bf(np.random.standard_normal((B, CQ, H, W)) * s[None, :, None, None]),
            "reference_features": bf(np.random.standard_normal((B, CR, H, W)) * r[None, :, None, None]),
            "Wq": bf(np.random.standard_normal((HID, CQ)) * 0.4 / np.sqrt(CQ) * t[:, None] / s[None, :]),
            "bq": bf(np.random.standard_normal(HID) * 0.1 * t),
            "Wk": bf(np.random.standard_normal((HID, CR)) * 0.4 / np.sqrt(CR) / t[:, None] / r[None, :]),
            "bk": bf(np.random.standard_normal(HID) * 0.1 / t)}


def reference(query_features, reference_features, Wq, bq, Wk, bk):
    xq = f64(query_features).reshape(B, CQ, P)
    xr = f64(reference_features).reshape(B, CR, P)
    Q = (mxq(f64(Wq), 1, "e4m3") @ mxq(xq, 1, "e4m3")) + f64(bq)[None, :, None]
    K = (mxq(f64(Wk), 1, "e4m3") @ mxq(xr, 1, "e4m3")) + f64(bk)[None, :, None]
    attn = mxq(Q, 1, "e4m3").transpose(0, 2, 1) @ mxq(K, 1, "e4m3")
    return attn.reshape(B, H, W, P)

@@ -1,0 +1,192 @@
+from contextlib import ExitStack
+
+import concourse.mybir as mybir
+from concourse.masks import make_identity
+
+BF16 = mybir.dt.bfloat16
+F32 = mybir.dt.float32
+U32 = mybir.dt.uint32
+U8 = mybir.dt.uint8
+FP8X4 = mybir.dt.float8_e4m3fn_x4
+
+P = 128
+PACK = 4
+K_PASS = P * PACK
+
+BATCH = 2
+CQ = 1024
+CR = 512
+HID = 512
+PIX = 512
+CHUNK = 128
+CHUNKS = PIX // CHUNK
+Q_PASSES = CQ // K_PASS
+
+FLOPS = 2 * BATCH * PIX * (HID * CQ + HID * CR + HID * PIX)
+
+
+def regroup_channels(copy, grouped, rows):
+    copy(
+        out=grouped.rearrange("q (c i) j -> q c j i", i=4),
+        in_=rows.rearrange("q j (c i) -> q c j i", i=4),
+    )
+
+
+def transpose_weight(nc, psum_w, ident, w_rows, w_grouped, passes):
+    words = w_rows[:].bitcast(F32).rearrange("p (t g q u) -> p t g u q", t=PACK, g=passes, u=2)
+    grouped_words = w_grouped[:].bitcast(F32).rearrange("q (g t p u) -> q g t p u", g=passes, t=PACK, u=2)
+    for g in range(passes):
+        for t0 in range(0, PACK, 2):
+            bank = psum_w.tile([P, 2, 2, P], F32, name="w_bank")
+            for t in range(2):
+                for u in range(2):
+                    nc.tensor.transpose(bank[:, t, u, :], words[:, t0 + t, g, u, :], ident[:])
+            nc.scalar.copy(
+                out=grouped_words[:, g, t0 : t0 + 2, :, :],
+                in_=bank[:].rearrange("q t u p -> q t p u"),
+            )
+
+
+def tile_crossattentionvaluefuser_pa_kernel(
+    tc, query_features, reference_features, Wq, bq, Wk, bk, out
+):
+    nc = tc.nc
+    with ExitStack() as ctx:
+        keep = ctx.enter_context(tc.tile_pool(name="keep", bufs=1))
+        stage = ctx.enter_context(tc.tile_pool(name="stage", bufs=4))
+        psum_w = ctx.enter_context(tc.psum_pool(name="psum_w", bufs=2))
+        psum_proj = ctx.enter_context(tc.psum_pool(name="psum_proj", bufs=3))
+        psum_logits = ctx.enter_context(tc.psum_pool(name="psum_logits", bufs=3))
+
+        xr_rows = [keep.tile([P, PACK * PIX], BF16, name="xr_rows%d" % b) for b in range(BATCH)]
+        xq_rows = [keep.tile([P, Q_PASSES * PACK * PIX], BF16, name="xq_rows%d" % b) for b in range(BATCH)]
+        wk_rows = keep.tile([P, PACK * CR], BF16)
+        wq_rows = keep.tile([P, PACK * CQ], BF16)
+        bk_sb = keep.tile([P, PACK], BF16)
+        bq_sb = keep.tile([P, PACK], BF16)
+
+        def load_xr(b):
+            nc.sync.dma_start(
+                out=xr_rows[b][:],
+                in_=reference_features[b].rearrange("(q j) h w -> q (j h w)", j=PACK),
+            )
+
+        def load_xq(b):
+            nc.sync.dma_start(
+                out=xq_rows[b][:].rearrange("q (g f) -> q g f", g=Q_PASSES),
+                in_=query_features[b].rearrange("(g q j) h w -> q g (j h w)", g=Q_PASSES, j=PACK),
+            )
+
+        load_xr(0)
+        nc.sync.dma_start(out=wk_rows[:], in_=Wk.rearrange("(p t) c -> p (t c)", t=PACK))
+        nc.sync.dma_start(out=wq_rows[:], in_=Wq.rearrange("(p t) c -> p (t c)", t=PACK))
+        load_xq(0)
+        load_xr(1)
+        load_xq(1)
+        nc.scalar.dma_start(out=bk_sb[:], in_=bk.rearrange("(p t) -> p t", t=PACK))
+        nc.scalar.dma_start(out=bq_sb[:], in_=bq.rearrange("(p t) -> p t", t=PACK))
+
+        ident = keep.tile([P, P], F32)
+        make_identity(nc, ident[:])
+
+        wk_grouped = keep.tile([P, PACK * HID], BF16, align_bytes=64)
+        wk_codes = keep.tile([P, HID], U32, align_bytes=64)
+        wk_scales = keep.tile([P, HID], U8, align_bytes=64)
+        wq_grouped = keep.tile([P, Q_PASSES * PACK * HID], BF16, align_bytes=64)
+        wq_codes = keep.tile([P, Q_PASSES * HID], U32, align_bytes=64)
+        wq_scales = keep.tile([P, Q_PASSES * HID], U8, align_bytes=64)
+
+        def regroup_copy(r):
+            return nc.vector.tensor_copy if r == 0 else nc.scalar.copy
+
+        def project(bank, w_codes, w_scales, x_codes, x_scales, passes):
+            for t in range(PACK):
+                for g in range(passes):
+                    w_cols = slice(g * HID + t * P, g * HID + (t + 1) * P)
+                    x_cols = slice(g * CHUNK, (g + 1) * CHUNK)
+                    nc.tensor.matmul_mx(
+                        out=bank[:, t, :],
+                        lhsT=w_codes[:, w_cols].bitcast(FP8X4),
+                        lhsT_scale=w_scales[:, w_cols],
+                        rhs=x_codes[:, x_cols].bitcast(FP8X4),
+                        rhs_scale=x_scales[:, x_cols],
+                        start=(g == 0),
+                        stop=(g == passes - 1),
+                    )
+
+        def add_bias(grouped, bank, bias):
+            nc.vector.tensor_tensor(
+                out=grouped.rearrange("p (n t) -> p n t", t=PACK),
+                in0=bank[:].rearrange("p t n -> p n t"),
+                in1=bias[:].unsqueeze(1).to_broadcast([P, CHUNK, PACK]),
+                op=mybir.AluOpType.add,
+            )
+
+        transpose_weight(nc, psum_w, ident, wk_rows, wk_grouped, 1)
+        nc.vector.quantize_mx(out=wk_codes[:].bitcast(FP8X4), scales=wk_scales[:], in_=wk_grouped[:])
+        transpose_weight(nc, psum_w, ident, wq_rows, wq_grouped, Q_PASSES)
+        for g in range(Q_PASSES):
+            nc.vector.quantize_mx(
+                out=wq_codes[:, g * HID : (g + 1) * HID].bitcast(FP8X4),
+                scales=wq_scales[:, g * HID : (g + 1) * HID],
+                in_=wq_grouped[:, g * PACK * HID : (g + 1) * PACK * HID],
+            )
+
+        for b in range(BATCH):
+            xr_grouped = keep.tile([P, PACK * PIX], BF16, name="xr_grouped%d" % b, align_bytes=64)
+            xr_codes = keep.tile([P, PIX], U32, name="xr_codes%d" % b, align_bytes=64)
+            xr_scales = keep.tile([P, PIX], U8, name="xr_scales%d" % b, align_bytes=64)
+            k_grouped = keep.tile([P, PACK * PIX], BF16, name="k_grouped%d" % b, align_bytes=64)
+            k_codes = keep.tile([P, PIX], U32, name="k_codes%d" % b, align_bytes=64)
+            k_scales = keep.tile([P, PIX], U8, name="k_scales%d" % b, align_bytes=64)
+            for r in range(CHUNKS):
+                pixels = slice(r * CHUNK, (r + 1) * CHUNK)
+                regroup_channels(
+                    regroup_copy(r),
+                    xr_grouped[:].rearrange("q (n j) -> q n j", j=PACK)[:, pixels, :],
+                    xr_rows[b][:].rearrange("q (j n) -> q j n", j=PACK)[:, :, pixels],
+                )
+            nc.vector.quantize_mx(out=xr_codes[:].bitcast(FP8X4), scales=xr_scales[:], in_=xr_grouped[:])
+            for r in range(CHUNKS):
+                pixels = slice(r * CHUNK, (r + 1) * CHUNK)
+                k_bank = psum_proj.tile([P, PACK, CHUNK], F32, name="proj_bank")
+                project(k_bank, wk_codes, wk_scales, xr_codes[:, pixels], xr_scales[:, pixels], 1)
+                add_bias(k_grouped[:, r * PACK * CHUNK : (r + 1) * PACK * CHUNK], k_bank, bk_sb)
+            nc.vector.quantize_mx(out=k_codes[:].bitcast(FP8X4), scales=k_scales[:], in_=k_grouped[:])
+
+            out_rows = out[b].rearrange("h w p -> (h w) p")
+            for r in range(CHUNKS):
+                pixels = slice(r * CHUNK, (r + 1) * CHUNK)
+                xq_grouped = keep.tile(
+                    [P, Q_PASSES * PACK * CHUNK], BF16, name="xq_grouped%d_%d" % (b, r), align_bytes=64
+                )
+                xq_codes = keep.tile([P, Q_PASSES * CHUNK], U32, name="xq_codes%d_%d" % (b, r), align_bytes=64)
+                xq_scales = keep.tile([P, Q_PASSES * CHUNK], U8, name="xq_scales%d_%d" % (b, r), align_bytes=64)
+                q_grouped = keep.tile([P, PACK * CHUNK], BF16, name="q_grouped%d_%d" % (b, r), align_bytes=64)
+                q_codes = keep.tile([P, CHUNK], U32, name="q_codes%d_%d" % (b, r), align_bytes=64)
+                q_scales = keep.tile([P, CHUNK], U8, name="q_scales%d_%d" % (b, r), align_bytes=64)
+                for g in range(Q_PASSES):
+                    regroup_channels(
+                        regroup_copy(r),
+                        xq_grouped[:].rearrange("q (g n j) -> q g n j", g=Q_PASSES, j=PACK)[:, g, :, :],
+                        xq_rows[b][:].rearrange("q (g j n) -> q g j n", g=Q_PASSES, j=PACK)[:, g, :, pixels],
+                    )
+                nc.vector.quantize_mx(out=xq_codes[:].bitcast(FP8X4), scales=xq_scales[:], in_=xq_grouped[:])
+                q_bank = psum_proj.tile([P, PACK, CHUNK], F32, name="proj_bank")
+                project(q_bank, wq_codes, wq_scales, xq_codes, xq_scales, Q_PASSES)
+                add_bias(q_grouped[:], q_bank, bq_sb)
+                nc.vector.quantize_mx(out=q_codes[:].bitcast(FP8X4), scales=q_scales[:], in_=q_grouped[:])
+
+                logits_bank = psum_logits.tile([P, PIX], F32, name="logits_bank")
+                nc.tensor.matmul_mx(
+                    out=logits_bank[:],
+                    lhsT=q_codes[:].bitcast(FP8X4),
+                    lhsT_scale=q_scales[:],
+                    rhs=k_codes[:].bitcast(FP8X4),
+                    rhs_scale=k_scales[:],
+                    start=True,
+                    stop=True,
+                )
+                logits = stage.tile([P, PIX], F32, name="logits")
+                nc.scalar.copy(out=logits[:], in_=logits_bank[:])
+                nc.sync.dma_start(out=out_rows[pixels, :], in_=logits[:])

@@ -20,9 +20,18 @@ HID = 512
 PIX = 512
 CHUNK = 128
 CHUNKS = PIX // CHUNK
+HALF = 256
+HALVES = PIX // HALF
 Q_PASSES = CQ // K_PASS
 
 FLOPS = 2 * BATCH * PIX * (HID * CQ + HID * CR + HID * PIX)
+
+
+STEPS = BATCH * CHUNKS
+PIECES = BATCH * HALVES * Q_PASSES
+PROJECT_AHEAD = 3
+QUANTISE_AHEAD = 2
+XR1_VECTOR_PIXELS = 256
 
 
 def regroup_channels(copy, grouped, rows):
@@ -32,31 +41,15 @@ def regroup_channels(copy, grouped, rows):
     )
 
 
-def transpose_weight(nc, psum_w, ident, w_rows, w_grouped, passes):
-    words = w_rows[:].bitcast(F32).rearrange("p (t g q u) -> p t g u q", t=PACK, g=passes, u=2)
-    grouped_words = w_grouped[:].bitcast(F32).rearrange("q (g t p u) -> q g t p u", g=passes, t=PACK, u=2)
-    for g in range(passes):
-        for t0 in range(0, PACK, 2):
-            bank = psum_w.tile([P, 2, 2, P], F32, name="w_bank")
-            for t in range(2):
-                for u in range(2):
-                    nc.tensor.transpose(bank[:, t, u, :], words[:, t0 + t, g, u, :], ident[:])
-            nc.scalar.copy(
-                out=grouped_words[:, g, t0 : t0 + 2, :, :],
-                in_=bank[:].rearrange("q t u p -> q t p u"),
-            )
-
-
 def tile_crossattentionvaluefuser_pa_kernel(
     tc, query_features, reference_features, Wq, bq, Wk, bk, out
 ):
     nc = tc.nc
     with ExitStack() as ctx:
         keep = ctx.enter_context(tc.tile_pool(name="keep", bufs=1))
-        stage = ctx.enter_context(tc.tile_pool(name="stage", bufs=4))
-        psum_w = ctx.enter_context(tc.psum_pool(name="psum_w", bufs=2))
-        psum_proj = ctx.enter_context(tc.psum_pool(name="psum_proj", bufs=3))
-        psum_logits = ctx.enter_context(tc.psum_pool(name="psum_logits", bufs=3))
+        psum_proj = ctx.enter_context(tc.psum_pool(name="psum_proj", bufs=4))
+        psum_other = ctx.enter_context(tc.psum_pool(name="psum_other", bufs=4))
+        ctx.enter_context(tc.manual_schedule())
 
         xr_rows = [keep.tile([P, PACK * PIX], BF16, name="xr_rows%d" % b) for b in range(BATCH)]
         xq_rows = [keep.tile([P, Q_PASSES * PACK * PIX], BF16, name="xq_rows%d" % b) for b in range(BATCH)]
@@ -77,11 +70,11 @@ def tile_crossattentionvaluefuser_pa_kernel(
                 in_=query_features[b].rearrange("(g q j) h w -> q g (j h w)", g=Q_PASSES, j=PACK),
             )
 
-        load_xr(0)
         nc.sync.dma_start(out=wk_rows[:], in_=Wk.rearrange("(p t) c -> p (t c)", t=PACK))
-        nc.sync.dma_start(out=wq_rows[:], in_=Wq.rearrange("(p t) c -> p (t c)", t=PACK))
-        load_xq(0)
+        load_xr(0)
         load_xr(1)
+        load_xq(0)
+        nc.sync.dma_start(out=wq_rows[:], in_=Wq.rearrange("(p t) c -> p (t c)", t=PACK))
         load_xq(1)
         nc.scalar.dma_start(out=bk_sb[:], in_=bk.rearrange("(p t) -> p t", t=PACK))
         nc.scalar.dma_start(out=bq_sb[:], in_=bq.rearrange("(p t) -> p t", t=PACK))
@@ -89,30 +82,78 @@ def tile_crossattentionvaluefuser_pa_kernel(
         ident = keep.tile([P, P], F32)
         make_identity(nc, ident[:])
 
-        wk_grouped = keep.tile([P, PACK * HID], BF16, align_bytes=64)
-        wk_codes = keep.tile([P, HID], U32, align_bytes=64)
-        wk_scales = keep.tile([P, HID], U8, align_bytes=64)
-        wq_grouped = keep.tile([P, Q_PASSES * PACK * HID], BF16, align_bytes=64)
-        wq_codes = keep.tile([P, Q_PASSES * HID], U32, align_bytes=64)
-        wq_scales = keep.tile([P, Q_PASSES * HID], U8, align_bytes=64)
+        def mx_tiles(name, columns):
+            grouped = keep.tile([P, PACK * columns], BF16, name=name + "_grouped", align_bytes=64)
+            codes = keep.tile([P, columns], U32, name=name + "_codes", align_bytes=64)
+            scales = keep.tile([P, columns], U8, name=name + "_scales", align_bytes=64)
+            return grouped, codes, scales
 
-        def regroup_copy(r):
-            return nc.vector.tensor_copy if r == 0 else nc.scalar.copy
+        def quantise(tiles, first=0, columns=None):
+            grouped, codes, scales = tiles
+            last = first + (columns or codes.shape[1])
+            nc.vector.quantize_mx(
+                out=codes[:, first:last].bitcast(FP8X4),
+                scales=scales[:, first:last],
+                in_=grouped[:, PACK * first : PACK * last],
+            )
 
-        def project(bank, w_codes, w_scales, x_codes, x_scales, passes):
+        wk = mx_tiles("wk", HID)
+        wq = mx_tiles("wq", Q_PASSES * HID)
+        xr = [mx_tiles("xr%d" % b, PIX) for b in range(BATCH)]
+        k_mx = [mx_tiles("k%d" % b, PIX) for b in range(BATCH)]
+        xq = [mx_tiles("xq%d" % h, Q_PASSES * HALF) for h in range(BATCH * HALVES)]
+        q_mx = [mx_tiles("q%d" % i, CHUNK) for i in range(STEPS)]
+
+        def transpose_weight(w_rows, w_grouped, passes):
+            words = w_rows[:].bitcast(F32).rearrange("p (t g q u) -> p t g u q", t=PACK, g=passes, u=2)
+            grouped_words = w_grouped[:].bitcast(F32).rearrange(
+                "q (g t p u) -> q g t p u", g=passes, t=PACK, u=2
+            )
+            for g in range(passes):
+                for t0 in range(0, PACK, 2):
+                    bank = psum_other.tile([P, 2, 2, P], F32, name="w_bank", tag="other")
+                    for t in range(2):
+                        for u in range(2):
+                            nc.tensor.transpose(bank[:, t, u, :], words[:, t0 + t, g, u, :], ident[:])
+                    nc.scalar.copy(
+                        out=grouped_words[:, g, t0 : t0 + 2, :, :],
+                        in_=bank[:].rearrange("q t u p -> q t p u"),
+                    )
+
+        def regroup_xr(copy, b, first, last):
+            regroup_channels(
+                copy,
+                xr[b][0][:].rearrange("q (n j) -> q n j", j=PACK)[:, first:last, :],
+                xr_rows[b][:].rearrange("q (j n) -> q j n", j=PACK)[:, :, first:last],
+            )
+
+        def regroup_xq(piece):
+            h, g = piece // Q_PASSES, piece % Q_PASSES
+            first = h % HALVES * HALF
+            regroup_channels(
+                nc.scalar.copy,
+                xq[h][0][:].rearrange("q (g n j) -> q g n j", g=Q_PASSES, j=PACK)[:, g, :, :],
+                xq_rows[h // HALVES][:].rearrange("q (g j n) -> q g j n", g=Q_PASSES, j=PACK)[
+                    :, g, :, first : first + HALF
+                ],
+            )
+
+        def project(w, x, first, stride, passes):
+            bank = psum_proj.tile([P, PACK, CHUNK], F32, name="proj_bank")
             for t in range(PACK):
                 for g in range(passes):
                     w_cols = slice(g * HID + t * P, g * HID + (t + 1) * P)
-                    x_cols = slice(g * CHUNK, (g + 1) * CHUNK)
+                    x_cols = slice(first + g * stride, first + g * stride + CHUNK)
                     nc.tensor.matmul_mx(
                         out=bank[:, t, :],
-                        lhsT=w_codes[:, w_cols].bitcast(FP8X4),
-                        lhsT_scale=w_scales[:, w_cols],
-                        rhs=x_codes[:, x_cols].bitcast(FP8X4),
-                        rhs_scale=x_scales[:, x_cols],
+                        lhsT=w[1][:, w_cols].bitcast(FP8X4),
+                        lhsT_scale=w[2][:, w_cols],
+                        rhs=x[1][:, x_cols].bitcast(FP8X4),
+                        rhs_scale=x[2][:, x_cols],
                         start=(g == 0),
                         stop=(g == passes - 1),
                     )
+            return bank
 
         def add_bias(grouped, bank, bias):
             nc.vector.tensor_tensor(
@@ -122,71 +163,69 @@ def tile_crossattentionvaluefuser_pa_kernel(
                 op=mybir.AluOpType.add,
             )
 
-        transpose_weight(nc, psum_w, ident, wk_rows, wk_grouped, 1)
-        nc.vector.quantize_mx(out=wk_codes[:].bitcast(FP8X4), scales=wk_scales[:], in_=wk_grouped[:])
-        transpose_weight(nc, psum_w, ident, wq_rows, wq_grouped, Q_PASSES)
-        for g in range(Q_PASSES):
-            nc.vector.quantize_mx(
-                out=wq_codes[:, g * HID : (g + 1) * HID].bitcast(FP8X4),
-                scales=wq_scales[:, g * HID : (g + 1) * HID],
-                in_=wq_grouped[:, g * PACK * HID : (g + 1) * PACK * HID],
+        def project_k(i):
+            return project(wk, xr[i // CHUNKS], i % CHUNKS * CHUNK, 0, 1)
+
+        def finish_k(i, bank):
+            first = i % CHUNKS * PACK * CHUNK
+            add_bias(k_mx[i // CHUNKS][0][:, first : first + PACK * CHUNK], bank, bk_sb)
+
+        def project_q(i):
+            return project(wq, xq[i * CHUNK // HALF], i * CHUNK % HALF, HALF, Q_PASSES)
+
+        def logits(i):
+            b, r = i // CHUNKS, i % CHUNKS
+            bank = psum_other.tile([P, PIX], F32, name="logits_bank", tag="other")
+            nc.tensor.matmul_mx(
+                out=bank[:],
+                lhsT=q_mx[i][1][:].bitcast(FP8X4),
+                lhsT_scale=q_mx[i][2][:],
+                rhs=k_mx[b][1][:].bitcast(FP8X4),
+                rhs_scale=k_mx[b][2][:],
+                start=True,
+                stop=True,
+            )
+            rows = keep.tile([P, PIX], F32, name="logits%d" % i)
+            nc.scalar.copy(out=rows[:], in_=bank[:])
+            nc.sync.dma_start(
+                out=out[b].rearrange("h w p -> (h w) p")[r * CHUNK : (r + 1) * CHUNK, :], in_=rows[:]
             )
 
-        for b in range(BATCH):
-            xr_grouped = keep.tile([P, PACK * PIX], BF16, name="xr_grouped%d" % b, align_bytes=64)
-            xr_codes = keep.tile([P, PIX], U32, name="xr_codes%d" % b, align_bytes=64)
-            xr_scales = keep.tile([P, PIX], U8, name="xr_scales%d" % b, align_bytes=64)
-            k_grouped = keep.tile([P, PACK * PIX], BF16, name="k_grouped%d" % b, align_bytes=64)
-            k_codes = keep.tile([P, PIX], U32, name="k_codes%d" % b, align_bytes=64)
-            k_scales = keep.tile([P, PIX], U8, name="k_scales%d" % b, align_bytes=64)
-            for r in range(CHUNKS):
-                pixels = slice(r * CHUNK, (r + 1) * CHUNK)
-                regroup_channels(
-                    regroup_copy(r),
-                    xr_grouped[:].rearrange("q (n j) -> q n j", j=PACK)[:, pixels, :],
-                    xr_rows[b][:].rearrange("q (j n) -> q j n", j=PACK)[:, :, pixels],
-                )
-            nc.vector.quantize_mx(out=xr_codes[:].bitcast(FP8X4), scales=xr_scales[:], in_=xr_grouped[:])
-            for r in range(CHUNKS):
-                pixels = slice(r * CHUNK, (r + 1) * CHUNK)
-                k_bank = psum_proj.tile([P, PACK, CHUNK], F32, name="proj_bank")
-                project(k_bank, wk_codes, wk_scales, xr_codes[:, pixels], xr_scales[:, pixels], 1)
-                add_bias(k_grouped[:, r * PACK * CHUNK : (r + 1) * PACK * CHUNK], k_bank, bk_sb)
-            nc.vector.quantize_mx(out=k_codes[:].bitcast(FP8X4), scales=k_scales[:], in_=k_grouped[:])
+        transpose_weight(wk_rows, wk[0], 1)
+        regroup_xr(nc.vector.tensor_copy, 0, 0, PIX)
+        quantise(xr[0])
+        regroup_xr(nc.vector.tensor_copy, 1, 0, XR1_VECTOR_PIXELS)
+        regroup_xr(nc.scalar.copy, 1, XR1_VECTOR_PIXELS, PIX)
+        quantise(wk)
+        quantise(xr[1])
+        for piece in range(PIECES // 2):
+            regroup_xq(piece)
 
-            out_rows = out[b].rearrange("h w p -> (h w) p")
-            for r in range(CHUNKS):
-                pixels = slice(r * CHUNK, (r + 1) * CHUNK)
-                xq_grouped = keep.tile(
-                    [P, Q_PASSES * PACK * CHUNK], BF16, name="xq_grouped%d_%d" % (b, r), align_bytes=64
-                )
-                xq_codes = keep.tile([P, Q_PASSES * CHUNK], U32, name="xq_codes%d_%d" % (b, r), align_bytes=64)
-                xq_scales = keep.tile([P, Q_PASSES * CHUNK], U8, name="xq_scales%d_%d" % (b, r), align_bytes=64)
-                q_grouped = keep.tile([P, PACK * CHUNK], BF16, name="q_grouped%d_%d" % (b, r), align_bytes=64)
-                q_codes = keep.tile([P, CHUNK], U32, name="q_codes%d_%d" % (b, r), align_bytes=64)
-                q_scales = keep.tile([P, CHUNK], U8, name="q_scales%d_%d" % (b, r), align_bytes=64)
-                for g in range(Q_PASSES):
-                    regroup_channels(
-                        regroup_copy(r),
-                        xq_grouped[:].rearrange("q (g n j) -> q g n j", g=Q_PASSES, j=PACK)[:, g, :, :],
-                        xq_rows[b][:].rearrange("q (g j n) -> q g j n", g=Q_PASSES, j=PACK)[:, g, :, pixels],
-                    )
-                nc.vector.quantize_mx(out=xq_codes[:].bitcast(FP8X4), scales=xq_scales[:], in_=xq_grouped[:])
-                q_bank = psum_proj.tile([P, PACK, CHUNK], F32, name="proj_bank")
-                project(q_bank, wq_codes, wq_scales, xq_codes, xq_scales, Q_PASSES)
-                add_bias(q_grouped[:], q_bank, bq_sb)
-                nc.vector.quantize_mx(out=q_codes[:].bitcast(FP8X4), scales=q_scales[:], in_=q_grouped[:])
+        k_banks = [project_k(i) for i in range(CHUNKS)]
+        for i in range(CHUNKS):
+            finish_k(i, k_banks[i])
+            k_banks.append(project_k(CHUNKS + i))
+        transpose_weight(wq_rows, wq[0], Q_PASSES)
+        for piece in range(PIECES // 2, PIECES):
+            regroup_xq(piece)
+        finish_k(CHUNKS, k_banks[CHUNKS])
+        quantise(k_mx[0])
+        for i in range(CHUNKS + 1, STEPS):
+            finish_k(i, k_banks[i])
+        for g in range(Q_PASSES):
+            quantise(wq, g * HID, HID)
+        for h in range(QUANTISE_AHEAD):
+            quantise(xq[h])
+        quantise(k_mx[1])
 
-                logits_bank = psum_logits.tile([P, PIX], F32, name="logits_bank")
-                nc.tensor.matmul_mx(
-                    out=logits_bank[:],
-                    lhsT=q_codes[:].bitcast(FP8X4),
-                    lhsT_scale=q_scales[:],
-                    rhs=k_codes[:].bitcast(FP8X4),
-                    rhs_scale=k_scales[:],
-                    start=True,
-                    stop=True,
-                )
-                logits = stage.tile([P, PIX], F32, name="logits")
-                nc.scalar.copy(out=logits[:], in_=logits_bank[:])
-                nc.sync.dma_start(out=out_rows[pixels, :], in_=logits[:])
+        q_banks = [project_q(i) for i in range(PROJECT_AHEAD)]
+        for i in range(STEPS + 1):
+            if i + PROJECT_AHEAD < STEPS:
+                q_banks.append(project_q(i + PROJECT_AHEAD))
+            if i < STEPS:
+                add_bias(q_mx[i][0][:], q_banks[i], bq_sb)
+            if i % 2 == 0 and i // 2 + QUANTISE_AHEAD < BATCH * HALVES:
+                quantise(xq[i // 2 + QUANTISE_AHEAD])
+            if i > 0:
+                quantise(q_mx[i - 1])
+                logits(i - 1)

@@ -186,7 +186,8 @@ def tile_crossattentionvaluefuser_pa_kernel(
                 stop=True,
             )
             rows = keep.tile([P, PIX], F32, name="logits%d" % i)
-            nc.scalar.copy(out=rows[:], in_=bank[:])
+            copy = nc.vector.tensor_copy if i == STEPS - 1 else nc.scalar.copy
+            copy(out=rows[:], in_=bank[:])
             nc.sync.dma_start(
                 out=out[b].rearrange("h w p -> (h w) p")[r * CHUNK : (r + 1) * CHUNK, :], in_=rows[:]
             )
@@ -194,9 +195,9 @@ def tile_crossattentionvaluefuser_pa_kernel(
         transpose_weight(wk_rows, wk[0], 1)
         regroup_xr(nc.vector.tensor_copy, 0, 0, PIX)
         quantise(xr[0])
+        quantise(wk)
         regroup_xr(nc.vector.tensor_copy, 1, 0, XR1_VECTOR_PIXELS)
         regroup_xr(nc.scalar.copy, 1, XR1_VECTOR_PIXELS, PIX)
-        quantise(wk)
         quantise(xr[1])
         for piece in range(PIECES // 2):
             regroup_xq(piece)
@@ -212,9 +213,10 @@ def tile_crossattentionvaluefuser_pa_kernel(
         quantise(k_mx[0])
         for i in range(CHUNKS + 1, STEPS):
             finish_k(i, k_banks[i])
+        quantise(xq[0])
         for g in range(Q_PASSES):
             quantise(wq, g * HID, HID)
-        for h in range(QUANTISE_AHEAD):
+        for h in range(1, QUANTISE_AHEAD):
             quantise(xq[h])
         quantise(k_mx[1])
 

from contextlib import ExitStack

import concourse.mybir as mybir
from concourse.masks import make_identity

BF16 = mybir.dt.bfloat16
F32 = mybir.dt.float32
U32 = mybir.dt.uint32
U8 = mybir.dt.uint8
FP8X4 = mybir.dt.float8_e4m3fn_x4

P = 128
PACK = 4
K_PASS = P * PACK

BATCH = 2
CQ = 1024
CR = 512
HID = 512
PIX = 512
CHUNK = 128
CHUNKS = PIX // CHUNK
HALF = 256
HALVES = PIX // HALF
Q_PASSES = CQ // K_PASS

FLOPS = 2 * BATCH * PIX * (HID * CQ + HID * CR + HID * PIX)


STEPS = BATCH * CHUNKS
PIECES = BATCH * HALVES * Q_PASSES
PROJECT_AHEAD = 3
QUANTISE_AHEAD = 2
XR1_VECTOR_PIXELS = 256


def regroup_channels(copy, grouped, rows):
    copy(
        out=grouped.rearrange("q (c i) j -> q c j i", i=4),
        in_=rows.rearrange("q j (c i) -> q c j i", i=4),
    )


def tile_crossattentionvaluefuser_pa_kernel(
    tc, query_features, reference_features, Wq, bq, Wk, bk, out
):
    nc = tc.nc
    with ExitStack() as ctx:
        keep = ctx.enter_context(tc.tile_pool(name="keep", bufs=1))
        psum_proj = ctx.enter_context(tc.psum_pool(name="psum_proj", bufs=4))
        psum_other = ctx.enter_context(tc.psum_pool(name="psum_other", bufs=4))
        ctx.enter_context(tc.manual_schedule())

        xr_rows = [keep.tile([P, PACK * PIX], BF16, name="xr_rows%d" % b) for b in range(BATCH)]
        xq_rows = [keep.tile([P, Q_PASSES * PACK * PIX], BF16, name="xq_rows%d" % b) for b in range(BATCH)]
        wk_rows = keep.tile([P, PACK * CR], BF16)
        wq_rows = keep.tile([P, PACK * CQ], BF16)
        bk_sb = keep.tile([P, PACK], BF16)
        bq_sb = keep.tile([P, PACK], BF16)

        def load_xr(b):
            nc.sync.dma_start(
                out=xr_rows[b][:],
                in_=reference_features[b].rearrange("(q j) h w -> q (j h w)", j=PACK),
            )

        def load_xq(b):
            nc.sync.dma_start(
                out=xq_rows[b][:].rearrange("q (g f) -> q g f", g=Q_PASSES),
                in_=query_features[b].rearrange("(g q j) h w -> q g (j h w)", g=Q_PASSES, j=PACK),
            )

        nc.sync.dma_start(out=wk_rows[:], in_=Wk.rearrange("(p t) c -> p (t c)", t=PACK))
        load_xr(0)
        load_xr(1)
        load_xq(0)
        nc.sync.dma_start(out=wq_rows[:], in_=Wq.rearrange("(p t) c -> p (t c)", t=PACK))
        load_xq(1)
        nc.scalar.dma_start(out=bk_sb[:], in_=bk.rearrange("(p t) -> p t", t=PACK))
        nc.scalar.dma_start(out=bq_sb[:], in_=bq.rearrange("(p t) -> p t", t=PACK))

        ident = keep.tile([P, P], F32)
        make_identity(nc, ident[:])

        def mx_tiles(name, columns):
            grouped = keep.tile([P, PACK * columns], BF16, name=name + "_grouped", align_bytes=64)
            codes = keep.tile([P, columns], U32, name=name + "_codes", align_bytes=64)
            scales = keep.tile([P, columns], U8, name=name + "_scales", align_bytes=64)
            return grouped, codes, scales

        def quantise(tiles, first=0, columns=None):
            grouped, codes, scales = tiles
            last = first + (columns or codes.shape[1])
            nc.vector.quantize_mx(
                out=codes[:, first:last].bitcast(FP8X4),
                scales=scales[:, first:last],
                in_=grouped[:, PACK * first : PACK * last],
            )

        wk = mx_tiles("wk", HID)
        wq = mx_tiles("wq", Q_PASSES * HID)
        xr = [mx_tiles("xr%d" % b, PIX) for b in range(BATCH)]
        k_mx = [mx_tiles("k%d" % b, PIX) for b in range(BATCH)]
        xq = [mx_tiles("xq%d" % h, Q_PASSES * HALF) for h in range(BATCH * HALVES)]
        q_mx = [mx_tiles("q%d" % i, CHUNK) for i in range(STEPS)]

        def transpose_weight(w_rows, w_grouped, passes):
            words = w_rows[:].bitcast(F32).rearrange("p (t g q u) -> p t g u q", t=PACK, g=passes, u=2)
            grouped_words = w_grouped[:].bitcast(F32).rearrange(
                "q (g t p u) -> q g t p u", g=passes, t=PACK, u=2
            )
            for g in range(passes):
                for t0 in range(0, PACK, 2):
                    bank = psum_other.tile([P, 2, 2, P], F32, name="w_bank", tag="other")
                    for t in range(2):
                        for u in range(2):
                            nc.tensor.transpose(bank[:, t, u, :], words[:, t0 + t, g, u, :], ident[:])
                    nc.scalar.copy(
                        out=grouped_words[:, g, t0 : t0 + 2, :, :],
                        in_=bank[:].rearrange("q t u p -> q t p u"),
                    )

        def regroup_xr(copy, b, first, last):
            regroup_channels(
                copy,
                xr[b][0][:].rearrange("q (n j) -> q n j", j=PACK)[:, first:last, :],
                xr_rows[b][:].rearrange("q (j n) -> q j n", j=PACK)[:, :, first:last],
            )

        def regroup_xq(piece):
            h, g = piece // Q_PASSES, piece % Q_PASSES
            first = h % HALVES * HALF
            regroup_channels(
                nc.scalar.copy,
                xq[h][0][:].rearrange("q (g n j) -> q g n j", g=Q_PASSES, j=PACK)[:, g, :, :],
                xq_rows[h // HALVES][:].rearrange("q (g j n) -> q g j n", g=Q_PASSES, j=PACK)[
                    :, g, :, first : first + HALF
                ],
            )

        def project(w, x, first, stride, passes):
            bank = psum_proj.tile([P, PACK, CHUNK], F32, name="proj_bank")
            for t in range(PACK):
                for g in range(passes):
                    w_cols = slice(g * HID + t * P, g * HID + (t + 1) * P)
                    x_cols = slice(first + g * stride, first + g * stride + CHUNK)
                    nc.tensor.matmul_mx(
                        out=bank[:, t, :],
                        lhsT=w[1][:, w_cols].bitcast(FP8X4),
                        lhsT_scale=w[2][:, w_cols],
                        rhs=x[1][:, x_cols].bitcast(FP8X4),
                        rhs_scale=x[2][:, x_cols],
                        start=(g == 0),
                        stop=(g == passes - 1),
                    )
            return bank

        def add_bias(grouped, bank, bias):
            nc.vector.tensor_tensor(
                out=grouped.rearrange("p (n t) -> p n t", t=PACK),
                in0=bank[:].rearrange("p t n -> p n t"),
                in1=bias[:].unsqueeze(1).to_broadcast([P, CHUNK, PACK]),
                op=mybir.AluOpType.add,
            )

        def project_k(i):
            return project(wk, xr[i // CHUNKS], i % CHUNKS * CHUNK, 0, 1)

        def finish_k(i, bank):
            first = i % CHUNKS * PACK * CHUNK
            add_bias(k_mx[i // CHUNKS][0][:, first : first + PACK * CHUNK], bank, bk_sb)

        def project_q(i):
            return project(wq, xq[i * CHUNK // HALF], i * CHUNK % HALF, HALF, Q_PASSES)

        def logits(i):
            b, r = i // CHUNKS, i % CHUNKS
            bank = psum_other.tile([P, PIX], F32, name="logits_bank", tag="other")
            nc.tensor.matmul_mx(
                out=bank[:],
                lhsT=q_mx[i][1][:].bitcast(FP8X4),
                lhsT_scale=q_mx[i][2][:],
                rhs=k_mx[b][1][:].bitcast(FP8X4),
                rhs_scale=k_mx[b][2][:],
                start=True,
                stop=True,
            )
            rows = keep.tile([P, PIX], F32, name="logits%d" % i)
            copy = nc.vector.tensor_copy if i == STEPS - 1 else nc.scalar.copy
            copy(out=rows[:], in_=bank[:])
            nc.sync.dma_start(
                out=out[b].rearrange("h w p -> (h w) p")[r * CHUNK : (r + 1) * CHUNK, :], in_=rows[:]
            )

        transpose_weight(wk_rows, wk[0], 1)
        regroup_xr(nc.vector.tensor_copy, 0, 0, PIX)
        quantise(xr[0])
        quantise(wk)
        regroup_xr(nc.vector.tensor_copy, 1, 0, XR1_VECTOR_PIXELS)
        regroup_xr(nc.scalar.copy, 1, XR1_VECTOR_PIXELS, PIX)
        quantise(xr[1])
        for piece in range(PIECES // 2):
            regroup_xq(piece)

        k_banks = [project_k(i) for i in range(CHUNKS)]
        for i in range(CHUNKS):
            finish_k(i, k_banks[i])
            k_banks.append(project_k(CHUNKS + i))
        transpose_weight(wq_rows, wq[0], Q_PASSES)
        for piece in range(PIECES // 2, PIECES):
            regroup_xq(piece)
        finish_k(CHUNKS, k_banks[CHUNKS])
        quantise(k_mx[0])
        for i in range(CHUNKS + 1, STEPS):
            finish_k(i, k_banks[i])
        quantise(xq[0])
        for g in range(Q_PASSES):
            quantise(wq, g * HID, HID)
        for h in range(1, QUANTISE_AHEAD):
            quantise(xq[h])
        quantise(k_mx[1])

        q_banks = [project_q(i) for i in range(PROJECT_AHEAD)]
        for i in range(STEPS + 1):
            if i + PROJECT_AHEAD < STEPS:
                q_banks.append(project_q(i + PROJECT_AHEAD))
            if i < STEPS:
                add_bias(q_mx[i][0][:], q_banks[i], bq_sb)
            if i % 2 == 0 and i // 2 + QUANTISE_AHEAD < BATCH * HALVES:
                quantise(xq[i // 2 + QUANTISE_AHEAD])
            if i > 0:
                quantise(q_mx[i - 1])
                logits(i - 1)
